import numpy as np
import ml_dtypes


def mxq(x, axis, fmt="e4m3"):
    dtype, down = {"e4m3": (ml_dtypes.float8_e4m3fn, 7), "e5m2": (ml_dtypes.float8_e5m2, 14)}[fmt]
    v = np.moveaxis(np.asarray(x, np.float32).astype(ml_dtypes.bfloat16).astype(np.float64), axis, -1)
    blocks = v.reshape(v.shape[:-1] + (-1, 32))
    amax = np.abs(blocks).max(-1, keepdims=True)
    byte = np.maximum(np.where(amax > 0, np.frexp(amax)[1] - 1 + 127, 0) - down, 1)
    scale = np.exp2(byte - 127.0)
    codes = (blocks / scale).astype(np.float32).astype(dtype).astype(np.float64)
    return np.moveaxis((codes * scale).reshape(v.shape), -1, axis)


WIDE = False


def mx_kscale(k):
    if not WIDE:
        return np.ones(k)
    levels = np.array([10, -10, 5, -5, 0])
    a = np.random.permutation(np.resize(levels, k // 512 * 4)).reshape(k // 512, 4)
    idx = np.arange(k)
    return np.exp2(a[idx // 512, idx % 128 // 32])


BF16 = ml_dtypes.bfloat16


def bf(x):
    return np.asarray(x, np.float32).astype(BF16)


def f64(x):
    return np.asarray(x).astype(np.float64)


E2M1 = np.array([0.0, 0.5, 1.0, 1.5, 2.0, 3.0, 4.0, 6.0, -0.0, -0.5, -1.0, -1.5, -2.0, -3.0, -4.0, -6.0])


def pack_weight(w, fmt):
    k, n = w.shape
    w = f64(bf(w)).reshape(k // 32, 32, n)
    amax = np.abs(w).max(1)
    if fmt == "e4m3":
        byte = np.frexp(amax)[1] - 1 + 127 - 7
    else:
        mant, ex = np.frexp(amax / 6.0)
        byte = np.where(mant > 0.5, ex, ex - 1) + 127
    byte = np.clip(np.where(amax > 0, byte, 1), 1, 254)
    scaled = (w * np.exp2(127.0 - byte)[:, None, :]).reshape(k, n).astype(np.float32)
    by_word = np.ascontiguousarray(scaled.reshape(k // 512, 128, 4, n).transpose(0, 1, 3, 2))
    if fmt == "e4m3":
        words = by_word.astype(ml_dtypes.float8_e4m3fn).view(np.uint8)
    else:
        c = by_word.astype(ml_dtypes.float4_e2m1fn).view(np.uint8) & 0xF
        words = c[..., 0::2] | (c[..., 1::2] << 4)
    return np.ascontiguousarray(words), np.ascontiguousarray(byte.astype(np.uint8).reshape(k // 512, 16, n))


def unpack_weight(words, scales, fmt):
    g, p, n, _ = words.shape
    if fmt == "e4m3":
        vals = np.ascontiguousarray(words).view(ml_dtypes.float8_e4m3fn).astype(np.float64)
    else:
        nib = np.empty((g, p, n, 4), np.uint8)
        nib[..., 0::2] = words & 0xF
        nib[..., 1::2] = words >> 4
        vals = E2M1[nib]
    vals = vals * np.repeat(np.exp2(scales.astype(np.float64) - 127.0), 8, axis=1)[..., None]
    return vals.transpose(0, 1, 3, 2).reshape(g * 512, n)

def pack4(w):
    words, scales = pack_weight(w, "e2m1")
    return words.reshape(words.shape[0], 128, -1), scales


def unpack4(words, scales):
    return unpack_weight(words.reshape(words.shape[0], 128, -1, 2), scales, "e2m1")


B, D, F0, F1, F2, F3, P = 512, 2048, 1024, 512, 256, 128, 200


def relu(v):
    return np.maximum(v, 0.0)


def neg_l1(feat, pr):
    return -np.stack([np.abs(feat - row).sum(-1) for row in pr], axis=1)


def setup_inputs():
    s = mx_kscale(F1)
    t = mx_kscale(F0)
    x = bf(np.random.standard_normal((B, D)))
    aW = np.random.standard_normal((D, D)) * 0.7 / np.sqrt(D)
    ab = bf(np.random.standard_normal(D) * 0.5)
    h_up = bf(np.maximum(np.random.standard_normal((B, F1)), 0.0) * 1.4 * s)
    h_skip = bf(np.maximum(np.random.standard_normal((B, F1)), 0.0) * 1.4 * s)
    Wu2 = np.random.standard_normal((F0, F1)) / np.sqrt(F1) / s[None, :] * t[:, None]
    bu2 = bf(np.random.standard_normal(F0) * 0.8 * t)
    Wu3 = np.random.standard_normal((D, F0)) * 1.4 / np.sqrt(F0) / t[None, :]
    bu3 = bf(np.random.standard_normal(D) * 0.8)
    protos = bf(np.random.standard_normal((P, D)))
    aW_words, aW_scales = pack4(np.ascontiguousarray(aW.T))
    Wu2_words, Wu2_scales = pack4(np.ascontiguousarray(Wu2.T))
    Wu3_words, Wu3_scales = pack4(np.ascontiguousarray(Wu3.T))
    return {
        "x": x,
        "aW_words": aW_words,
        "aW_scales": aW_scales,
        "ab": ab,
        "h_up": h_up,
        "h_skip": h_skip,
        "Wu2_words": Wu2_words,
        "Wu2_scales": Wu2_scales,
        "bu2": bu2,
        "Wu3_words": Wu3_words,
        "Wu3_scales": Wu3_scales,
        "bu3": bu3,
        "protos": protos,
    }


def reference(x, aW_words, aW_scales, ab, h_up, h_skip, Wu2_words, Wu2_scales, bu2, Wu3_words, Wu3_scales, bu3, protos):
    xf = f64(x)
    z = f64(h_up) + f64(h_skip)
    u2 = relu((mxq(z, 1, "e4m3") @ unpack4(Wu2_words, Wu2_scales)) + f64(bu2))
    u3 = relu((mxq(u2, 1, "e4m3") @ unpack4(Wu3_words, Wu3_scales)) + f64(bu3))
    feat = xf + ((mxq(xf, 1, "e4m3") @ unpack4(aW_words, aW_scales)) + f64(ab)) + u3
    return neg_l1(feat, f64(protos))

@@ -1,0 +1,347 @@
+from contextlib import ExitStack
+
+import concourse.mybir as mybir
+from concourse.masks import make_identity
+
+F32 = mybir.dt.float32
+BF16 = mybir.dt.bfloat16
+I32 = mybir.dt.int32
+U32 = mybir.dt.uint32
+U8 = mybir.dt.uint8
+FP8X4 = mybir.dt.float8_e4m3fn_x4
+FP4X4 = mybir.dt.float4_e2m1fn_x4
+ALU = mybir.AluOpType
+ACT = mybir.ActivationFunctionType
+AXIS = mybir.AxisListType
+
+P = 128
+PACK = 4
+K_PASS = P * PACK
+BANK = 512
+
+B, D, F0, F1, N_PROTO = 512, 2048, 1024, 512, 200
+N_BT = B // P
+N_CHUNK = D // P
+N_VEC = 8
+N_ACT = N_CHUNK - N_VEC
+N_PAIR = N_PROTO // 2
+
+FLOPS = 2 * B * (D * D + F1 * F0 + F0 * D) + 3 * B * N_PROTO * D
+
+
+def zero(nc, tile_ap):
+    nc.vector.memset(tile_ap.bitcast(I32), 0)
+
+
+def load_bytes(nc, tile_ap, dram_ap):
+    nc.sync.dma_start(out=tile_ap.bitcast(I32), in_=dram_ap.bitcast(I32))
+
+
+def load_scale_rows(nc, planes, scales):
+    for quadrant in range(4):
+        load_bytes(
+            nc,
+            planes[32 * quadrant : 32 * quadrant + 4, :, :],
+            scales[:, 4 * quadrant : 4 * quadrant + 4, :].rearrange("g r n -> r g n"),
+        )
+
+
+def quantise(nc, codes, plane, grouped_bf16):
+    nc.vector.quantize_mx(out=codes.bitcast(FP8X4), scales=plane, in_=grouped_bf16)
+
+
+def group_computed_rows(nc, turn_psum, ident_bf16, rows, k0, grouped):
+    for half in range(2):
+        turned = turn_psum.tile([P, PACK, 2 * P], BF16, tag="turn")
+        for t in range(PACK):
+            for i in range(2):
+                nc.tensor.transpose(
+                    turned[:, t, P * i : P * (i + 1)],
+                    rows[:, 2 * half + i, k0 + t : k0 + K_PASS : PACK],
+                    ident_bf16[:],
+                )
+        nc.vector.tensor_copy(
+            out=grouped[:, 2 * P * half : 2 * P * (half + 1), :],
+            in_=turned[:].rearrange("p t b -> p b t"),
+        )
+
+
+def build_features(tc, ins, ident_f32, feat_t, proto_vec, proto_act_half, proto_neg_half_sum):
+    nc = tc.nc
+    (x, aw_words, aw_scales, ab, h_up, h_skip, wu2_words, wu2_scales, bu2, wu3_words, wu3_scales, bu3, protos) = ins
+    with ExitStack() as ctx:
+        res = ctx.enter_context(tc.tile_pool(name="resident", bufs=1))
+        stage = ctx.enter_context(tc.tile_pool(name="stage", bufs=2))
+        turn_psum = ctx.enter_context(tc.psum_pool(name="turn_psum", bufs=3))
+        mm_psum = ctx.enter_context(tc.psum_pool(name="mm_psum", bufs=4))
+
+        ident_bf16 = res.tile([P, P], BF16)
+        make_identity(nc, ident_bf16[:])
+
+        wu2_s = res.tile([P, F1 // K_PASS, F0], U8, align_bytes=64)
+        aw_s = res.tile([P, D // K_PASS, D], U8, align_bytes=64)
+        wu3_s = res.tile([P, F0 // K_PASS, D], U8, align_bytes=64)
+        zero(nc, wu2_s[:])
+        zero(nc, aw_s[:])
+        zero(nc, wu3_s[:])
+        load_scale_rows(nc, wu2_s, wu2_scales)
+        load_scale_rows(nc, aw_s, aw_scales)
+        load_scale_rows(nc, wu3_s, wu3_scales)
+
+        h_up_sb = res.tile([P, N_BT, F1], BF16)
+        h_skip_sb = res.tile([P, N_BT, F1], BF16)
+        nc.sync.dma_start(out=h_up_sb[:], in_=h_up.rearrange("(t b) k -> b t k", b=P))
+        nc.sync.dma_start(out=h_skip_sb[:], in_=h_skip.rearrange("(t b) k -> b t k", b=P))
+        wu2_w = res.tile([P, 2 * F0], U8, align_bytes=64)
+        load_bytes(nc, wu2_w[:], wu2_words[0])
+        x_sb = res.tile([P, N_BT, D], BF16)
+        for bt in range(N_BT):
+            nc.sync.dma_start(out=x_sb[:, bt, :], in_=x[P * bt : P * (bt + 1), :])
+        bu2_all = res.tile([P, F0], BF16)
+        nc.sync.dma_start(out=bu2_all[:], in_=bu2.partition_broadcast(P))
+        bias_rows = res.tile([P, P], BF16)
+        zero(nc, bias_rows[:])
+        nc.sync.dma_start(out=bias_rows[0:N_CHUNK, :], in_=ab.rearrange("(c m) -> c m", m=P))
+        nc.sync.dma_start(out=bias_rows[N_CHUNK : 2 * N_CHUNK, :], in_=bu3.rearrange("(c m) -> c m", m=P))
+        aw_w = res.tile([P, D // K_PASS, 2 * D], U8, align_bytes=64)
+        for g in range(D // K_PASS):
+            load_bytes(nc, aw_w[:, g, :], aw_words[g])
+        wu3_w = res.tile([P, F0 // K_PASS, 2 * D], U8, align_bytes=64)
+        for g in range(F0 // K_PASS):
+            load_bytes(nc, wu3_w[:, g, :], wu3_words[g])
+        protos_sb = res.tile([P, 2, D], BF16)
+        zero(nc, protos_sb[:, 1, :])
+        nc.sync.dma_start(out=protos_sb[:, 0, :], in_=protos[0:P, :])
+        nc.sync.dma_start(out=protos_sb[0 : N_PROTO - P, 1, :], in_=protos[P:N_PROTO, :])
+
+        z_sb = res.tile([P, N_BT, F1], BF16)
+        nc.vector.tensor_tensor(out=z_sb[:], in0=h_up_sb[:], in1=h_skip_sb[:], op=ALU.add)
+        z_grouped = res.tile([P, B, PACK], BF16, align_bytes=64)
+        group_computed_rows(nc, turn_psum, ident_bf16, z_sb, 0, z_grouped)
+        z_codes = res.tile([P, B], U32, align_bytes=64)
+        z_plane = res.tile([P, B], U8, align_bytes=64)
+        quantise(nc, z_codes[:], z_plane[:], z_grouped[:].rearrange("p b t -> p (b t)"))
+
+        x_codes = res.tile([P, D // K_PASS, B], U32, align_bytes=64)
+        x_plane = res.tile([P, D // K_PASS, B], U8, align_bytes=64)
+        for g in range(D // K_PASS):
+            x_grouped = stage.tile([P, B, 2], F32, align_bytes=64)
+            for half in range(2):
+                turned = turn_psum.tile([P, 2, 2 * P], F32, tag="turn")
+                for u in range(2):
+                    for i in range(2):
+                        x_words = x_sb[:, 2 * half + i, :].bitcast(F32)
+                        nc.tensor.transpose(
+                            turned[:, u, P * i : P * (i + 1)],
+                            x_words[:, 256 * g + u : 256 * (g + 1) : 2],
+                            ident_f32[:],
+                        )
+                nc.scalar.copy(
+                    out=x_grouped[:, 2 * P * half : 2 * P * (half + 1), :],
+                    in_=turned[:].rearrange("p u b -> p b u"),
+                )
+            quantise(
+                nc, x_codes[:, g, :], x_plane[:, g, :], x_grouped[:].rearrange("p b u -> p (b u)").bitcast(BF16)
+            )
+
+        u2_sb = res.tile([P, N_BT, F0], BF16)
+        for bt in range(N_BT):
+            for g in range(F0 // BANK):
+                n_cols = slice(BANK * g, BANK * (g + 1))
+                u2_ps = mm_psum.tile([P, BANK], F32, tag="mm")
+                nc.tensor.matmul_mx(
+                    out=u2_ps[:],
+                    lhsT=z_codes[:, P * bt : P * (bt + 1)].bitcast(FP8X4),
+                    lhsT_scale=z_plane[:, P * bt : P * (bt + 1)],
+                    rhs=wu2_w[:, 2 * BANK * g : 2 * BANK * (g + 1)].bitcast(FP4X4),
+                    rhs_scale=wu2_s[:, 0, n_cols],
+                    start=True,
+                    stop=True,
+                )
+                u2_biased = stage.tile([P, BANK], F32)
+                nc.vector.tensor_tensor(out=u2_biased[:], in0=u2_ps[:], in1=bu2_all[:, n_cols], op=ALU.add)
+                nc.scalar.activation(out=u2_sb[:, bt, n_cols], in_=u2_biased[:], func=ACT.Relu)
+
+        bias_ps = turn_psum.tile([P, P], BF16, tag="turn")
+        nc.tensor.transpose(bias_ps[:], bias_rows[:], ident_bf16[:])
+        bias_cols = res.tile([P, 2 * N_CHUNK], F32)
+        nc.vector.tensor_copy(out=bias_cols[:], in_=bias_ps[:, 0 : 2 * N_CHUNK])
+
+        for c in range(N_CHUNK):
+            xt_ps = turn_psum.tile([P, B], BF16, tag="turn")
+            for bt in range(N_BT):
+                nc.tensor.transpose(xt_ps[:, P * bt : P * (bt + 1)], x_sb[:, bt, P * c : P * (c + 1)], ident_bf16[:])
+            nc.scalar.activation(
+                out=feat_t[:, c, :], in_=xt_ps[:], func=ACT.Identity, bias=bias_cols[:, c : c + 1], scale=1.0
+            )
+
+        for quarter in range(N_CHUNK // 4):
+            pt_ps = turn_psum.tile([P, 4, 2 * P], BF16, tag="turn")
+            for i in range(4):
+                c = 4 * quarter + i
+                for h in range(2):
+                    nc.tensor.transpose(
+                        pt_ps[:, i, P * h : P * (h + 1)], protos_sb[:, h, P * c : P * (c + 1)], ident_bf16[:]
+                    )
+            c0 = 4 * quarter
+            if c0 < N_VEC:
+                nc.vector.tensor_copy(out=proto_vec[:, c0 : c0 + 4, :], in_=pt_ps[:, :, 0:N_PROTO])
+            else:
+                nc.vector.tensor_scalar(
+                    out=proto_act_half[:, c0 - N_VEC : c0 - N_VEC + 4, :],
+                    in0=pt_ps[:, :, 0:N_PROTO],
+                    scalar1=0.5,
+                    scalar2=None,
+                    op0=ALU.mult,
+                )
+        proto_sum = res.tile([P, N_PROTO], F32)
+        nc.vector.tensor_reduce(
+            out=proto_sum[:], in_=proto_vec[:].rearrange("m c p -> m p c"), axis=AXIS.X, op=ALU.add
+        )
+        nc.vector.tensor_scalar(
+            out=proto_neg_half_sum[:], in0=proto_sum[:], scalar1=-0.5, scalar2=None, op0=ALU.mult
+        )
+
+        u2_codes = res.tile([P, F0 // K_PASS, B], U32, align_bytes=64)
+        u2_plane = res.tile([P, F0 // K_PASS, B], U8, align_bytes=64)
+        for g in range(F0 // K_PASS):
+            u2_grouped = stage.tile([P, B, PACK], BF16, align_bytes=64)
+            group_computed_rows(nc, turn_psum, ident_bf16, u2_sb, K_PASS * g, u2_grouped)
+            quantise(nc, u2_codes[:, g, :], u2_plane[:, g, :], u2_grouped[:].rearrange("p b t -> p (b t)"))
+
+        for c in range(N_CHUNK):
+            a_ps = mm_psum.tile([P, B], F32, tag="mm")
+            for g in range(D // K_PASS):
+                nc.tensor.matmul_mx(
+                    out=a_ps[:],
+                    lhsT=aw_w[:, g, 2 * P * c : 2 * P * (c + 1)].bitcast(FP4X4),
+                    lhsT_scale=aw_s[:, g, P * c : P * (c + 1)],
+                    rhs=x_codes[:, g, :].bitcast(FP8X4),
+                    rhs_scale=x_plane[:, g, :],
+                    start=(g == 0),
+                    stop=(g == D // K_PASS - 1),
+                )
+            nc.vector.tensor_tensor(out=feat_t[:, c, :], in0=a_ps[:], in1=feat_t[:, c, :], op=ALU.add)
+
+        for c in range(N_CHUNK):
+            u3_ps = mm_psum.tile([P, B], F32, tag="mm")
+            for g in range(F0 // K_PASS):
+                nc.tensor.matmul_mx(
+                    out=u3_ps[:],
+                    lhsT=wu3_w[:, g, 2 * P * c : 2 * P * (c + 1)].bitcast(FP4X4),
+                    lhsT_scale=wu3_s[:, g, P * c : P * (c + 1)],
+                    rhs=u2_codes[:, g, :].bitcast(FP8X4),
+                    rhs_scale=u2_plane[:, g, :],
+                    start=(g == 0),
+                    stop=(g == F0 // K_PASS - 1),
+                )
+            u3 = stage.tile([P, B], F32)
+            nc.scalar.activation(
+                out=u3[:], in_=u3_ps[:], func=ACT.Relu, bias=bias_cols[:, N_CHUNK + c : N_CHUNK + c + 1], scale=1.0
+            )
+            nc.vector.tensor_tensor(out=feat_t[:, c, :], in0=u3[:], in1=feat_t[:, c, :], op=ALU.add)
+
+
+def add_turned(nc, ident_f32, turned, block_row, first, last):
+    for bt in range(N_BT):
+        nc.tensor.matmul(
+            out=turned[:, bt, :],
+            lhsT=block_row[:, P * bt : P * (bt + 1)],
+            rhs=ident_f32[:],
+            is_transpose=True,
+            start=(first and bt == 0),
+            stop=(last and bt == N_BT - 1),
+        )
+
+
+def sum_distances(tc, ident_f32, feat_t, proto_vec, proto_act_half, proto_neg_half_sum, out):
+    nc = tc.nc
+    with ExitStack() as ctx:
+        small = ctx.enter_context(tc.tile_pool(name="small", bufs=1))
+        act_pool = ctx.enter_context(tc.tile_pool(name="act_pool", bufs=8))
+        vec_pool = ctx.enter_context(tc.tile_pool(name="vec_pool", bufs=4))
+        bank_pool = ctx.enter_context(tc.psum_pool(name="bank_pool", bufs=6))
+
+        half_sum = small.tile([P, N_PROTO, N_BT], F32)
+
+        feat_sum = small.tile([P, B], F32)
+        nc.vector.tensor_reduce(
+            out=feat_sum[:], in_=feat_t[:, 0:N_VEC, :].rearrange("m c b -> m b c"), axis=AXIS.X, op=ALU.add
+        )
+        feat_turned = bank_pool.tile([P, N_BT, P], F32, tag="bank")
+        add_turned(nc, ident_f32, feat_turned, feat_sum, first=True, last=True)
+        feat_rowsum = small.tile([P, N_BT], F32)
+        nc.vector.tensor_reduce(out=feat_rowsum[:], in_=feat_turned[:], axis=AXIS.X, op=ALU.add)
+
+        with tc.manual_schedule():
+            waiting = []
+            for pair in range(N_PAIR + 1):
+                for p, max_sum, turned in waiting:
+                    add_turned(nc, ident_f32, turned, max_sum, first=False, last=True)
+                current = []
+                if pair < N_PAIR:
+                    for p in (2 * pair, 2 * pair + 1):
+                        turned = bank_pool.tile([P, N_BT, P], F32, tag="bank")
+                        for i in range(N_ACT):
+                            half_abs = act_pool.tile([P, B], F32)
+                            nc.scalar.activation(
+                                out=half_abs[:],
+                                in_=feat_t[:, N_VEC + i, :],
+                                func=ACT.Abs,
+                                bias=proto_act_half[:, i, p : p + 1],
+                                scale=-0.5,
+                            )
+                            add_turned(nc, ident_f32, turned, half_abs, first=(i == 0), last=False)
+                        max_sum = vec_pool.tile([P, B], F32)
+                        current.append((p, max_sum, turned))
+                    for c in range(N_VEC):
+                        for p, max_sum, turned in current:
+                            if c == 0:
+                                nc.vector.tensor_scalar(
+                                    out=max_sum[:],
+                                    in0=feat_t[:, c, :],
+                                    scalar1=proto_vec[:, c, p : p + 1],
+                                    scalar2=proto_neg_half_sum[:, p : p + 1],
+                                    op0=ALU.max,
+                                    op1=ALU.add,
+                                )
+                            else:
+                                nc.vector.scalar_tensor_tensor(
+                                    out=max_sum[:],
+                                    in0=feat_t[:, c, :],
+                                    scalar=proto_vec[:, c, p : p + 1],
+                                    in1=max_sum[:],
+                                    op0=ALU.max,
+                                    op1=ALU.add,
+                                )
+                for p, max_sum, turned in waiting:
+                    nc.vector.tensor_reduce(out=half_sum[:, p, :], in_=turned[:], axis=AXIS.X, op=ALU.add)
+                waiting = current
+
+        result = small.tile([P, N_BT, N_PROTO], F32)
+        for bt in range(N_BT):
+            nc.vector.tensor_scalar(
+                out=result[:, bt, :],
+                in0=half_sum[:, :, bt],
+                scalar1=-2.0,
+                scalar2=feat_rowsum[:, bt : bt + 1],
+                op0=ALU.mult,
+                op1=ALU.add,
+            )
+        nc.sync.dma_start(out=out.rearrange("(t b) p -> b t p", b=P), in_=result[:])
+
+
+def tile_prototypelearnerv4_pa_kernel(
+    tc, x, aW_words, aW_scales, ab, h_up, h_skip, Wu2_words, Wu2_scales, bu2, Wu3_words, Wu3_scales, bu3, protos, out
+):
+    nc = tc.nc
+    with tc.tile_pool(name="keep", bufs=1) as keep:
+        ident_f32 = keep.tile([P, P], F32)
+        make_identity(nc, ident_f32[:])
+        feat_t = keep.tile([P, N_CHUNK, B], F32)
+        proto_vec = keep.tile([P, N_VEC, N_PROTO], F32)
+        proto_act_half = keep.tile([P, N_ACT, N_PROTO], F32)
+        proto_neg_half_sum = keep.tile([P, N_PROTO], F32)
+        ins = (x, aW_words, aW_scales, ab, h_up, h_skip, Wu2_words, Wu2_scales, bu2, Wu3_words, Wu3_scales, bu3, protos)
+        build_features(tc, ins, ident_f32, feat_t, proto_vec, proto_act_half, proto_neg_half_sum)
+        sum_distances(tc, ident_f32, feat_t, proto_vec, proto_act_half, proto_neg_half_sum, out)

@@ -24,6 +24,7 @@ N_BT = B // P
 N_CHUNK = D // P
 N_VEC = 8
 N_ACT = N_CHUNK - N_VEC
+N_CHAIN = 7
 N_PAIR = N_PROTO // 2
 
 FLOPS = 2 * B * (D * D + F1 * F0 + F0 * D) + 3 * B * N_PROTO * D
@@ -276,13 +277,16 @@ def sum_distances(tc, ident_f32, feat_t, proto_vec, proto_act_half, proto_neg_ha
         with tc.manual_schedule():
             waiting = []
             for pair in range(N_PAIR + 1):
-                for p, max_sum, turned in waiting:
-                    add_turned(nc, ident_f32, turned, max_sum, first=False, last=True)
+                for p, vec_tiles, turned in waiting:
+                    for i, vec_tile in enumerate(vec_tiles):
+                        add_turned(nc, ident_f32, turned, vec_tile, first=False, last=(i == len(vec_tiles) - 1))
                 current = []
                 if pair < N_PAIR:
                     for p in (2 * pair, 2 * pair + 1):
                         turned = bank_pool.tile([P, N_BT, P], F32, tag="bank")
-                        for i in range(N_ACT):
+                        current.append((p, [], turned))
+                    for i in range(N_ACT):
+                        for p, vec_tiles, turned in current:
                             half_abs = act_pool.tile([P, B], F32)
                             nc.scalar.activation(
                                 out=half_abs[:],
@@ -292,29 +296,39 @@ def sum_distances(tc, ident_f32, feat_t, proto_vec, proto_act_half, proto_neg_ha
                                 scale=-0.5,
                             )
                             add_turned(nc, ident_f32, turned, half_abs, first=(i == 0), last=False)
+                    for p, vec_tiles, turned in current:
                         max_sum = vec_pool.tile([P, B], F32)
-                        current.append((p, max_sum, turned))
-                    for c in range(N_VEC):
-                        for p, max_sum, turned in current:
-                            if c == 0:
-                                nc.vector.tensor_scalar(
-                                    out=max_sum[:],
-                                    in0=feat_t[:, c, :],
-                                    scalar1=proto_vec[:, c, p : p + 1],
-                                    scalar2=proto_neg_half_sum[:, p : p + 1],
-                                    op0=ALU.max,
-                                    op1=ALU.add,
-                                )
-                            else:
-                                nc.vector.scalar_tensor_tensor(
-                                    out=max_sum[:],
-                                    in0=feat_t[:, c, :],
-                                    scalar=proto_vec[:, c, p : p + 1],
-                                    in1=max_sum[:],
-                                    op0=ALU.max,
-                                    op1=ALU.add,
-                                )
-                for p, max_sum, turned in waiting:
+                        nc.vector.tensor_scalar(
+                            out=max_sum[:],
+                            in0=feat_t[:, 0, :],
+                            scalar1=proto_vec[:, 0, p : p + 1],
+                            scalar2=proto_neg_half_sum[:, p : p + 1],
+                            op0=ALU.max,
+                            op1=ALU.add,
+                        )
+                        vec_tiles.append(max_sum)
+                    for c in range(1, N_CHAIN):
+                        for p, vec_tiles, turned in current:
+                            nc.vector.scalar_tensor_tensor(
+                                out=vec_tiles[0][:],
+                                in0=feat_t[:, c, :],
+                                scalar=proto_vec[:, c, p : p + 1],
+                                in1=vec_tiles[0][:],
+                                op0=ALU.max,
+                                op1=ALU.add,
+                            )
+                    for c in range(N_CHAIN, N_VEC):
+                        for p, vec_tiles, turned in current:
+                            max_alone = vec_pool.tile([P, B], F32)
+                            nc.vector.tensor_scalar(
+                                out=max_alone[:],
+                                in0=feat_t[:, c, :],
+                                scalar1=proto_vec[:, c, p : p + 1],
+                                scalar2=None,
+                                op0=ALU.max,
+                            )
+                            vec_tiles.append(max_alone)
+                for p, vec_tiles, turned in waiting:
                     nc.vector.tensor_reduce(out=half_sum[:, p, :], in_=turned[:], axis=AXIS.X, op=ALU.add)
                 waiting = current
 

@@ -22,9 +22,10 @@ BANK = 512
 B, D, F0, F1, N_PROTO = 512, 2048, 1024, 512, 200
 N_BT = B // P
 N_CHUNK = D // P
-N_VEC = 8
+N_CHAIN = 5
+N_ALONE = 5
+N_VEC = N_CHAIN + N_ALONE
 N_ACT = N_CHUNK - N_VEC
-N_CHAIN = 7
 N_PAIR = N_PROTO // 2
 
 FLOPS = 2 * B * (D * D + F1 * F0 + F0 * D) + 3 * B * N_PROTO * D
@@ -176,24 +177,15 @@ def build_features(tc, ins, ident_f32, feat_t, proto_vec, proto_act_half, proto_
                 out=feat_t[:, c, :], in_=xt_ps[:], func=ACT.Identity, bias=bias_cols[:, c : c + 1], scale=1.0
             )
 
-        for quarter in range(N_CHUNK // 4):
-            pt_ps = turn_psum.tile([P, 4, 2 * P], BF16, tag="turn")
-            for i in range(4):
-                c = 4 * quarter + i
-                for h in range(2):
-                    nc.tensor.transpose(
-                        pt_ps[:, i, P * h : P * (h + 1)], protos_sb[:, h, P * c : P * (c + 1)], ident_bf16[:]
-                    )
-            c0 = 4 * quarter
-            if c0 < N_VEC:
-                nc.vector.tensor_copy(out=proto_vec[:, c0 : c0 + 4, :], in_=pt_ps[:, :, 0:N_PROTO])
+        for c in range(N_CHUNK):
+            pt_ps = turn_psum.tile([P, 2 * P], BF16, tag="turn")
+            for h in range(2):
+                nc.tensor.transpose(pt_ps[:, P * h : P * (h + 1)], protos_sb[:, h, P * c : P * (c + 1)], ident_bf16[:])
+            if c < N_VEC:
+                nc.vector.tensor_copy(out=proto_vec[:, c, :], in_=pt_ps[:, 0:N_PROTO])
             else:
                 nc.vector.tensor_scalar(
-                    out=proto_act_half[:, c0 - N_VEC : c0 - N_VEC + 4, :],
-                    in0=pt_ps[:, :, 0:N_PROTO],
-                    scalar1=0.5,
-                    scalar2=None,
-                    op0=ALU.mult,
+                    out=proto_act_half[:, c - N_VEC, :], in0=pt_ps[:, 0:N_PROTO], scalar1=0.5, scalar2=None, op0=ALU.mult
                 )
         proto_sum = res.tile([P, N_PROTO], F32)
         nc.vector.tensor_reduce(
@@ -260,7 +252,9 @@ def sum_distances(tc, ident_f32, feat_t, proto_vec, proto_act_half, proto_neg_ha
     with ExitStack() as ctx:
         small = ctx.enter_context(tc.tile_pool(name="small", bufs=1))
         act_pool = ctx.enter_context(tc.tile_pool(name="act_pool", bufs=8))
-        vec_pool = ctx.enter_context(tc.tile_pool(name="vec_pool", bufs=4))
+        alone_pool = ctx.enter_context(tc.tile_pool(name="alone_pool", bufs=6))
+        sum_pool = ctx.enter_context(tc.tile_pool(name="sum_pool", bufs=4))
+        drop_pool = ctx.enter_context(tc.tile_pool(name="drop_pool", bufs=2))
         bank_pool = ctx.enter_context(tc.psum_pool(name="bank_pool", bufs=6))
 
         half_sum = small.tile([P, N_PROTO, N_BT], F32)
@@ -277,59 +271,62 @@ def sum_distances(tc, ident_f32, feat_t, proto_vec, proto_act_half, proto_neg_ha
         with tc.manual_schedule():
             waiting = []
             for pair in range(N_PAIR + 1):
-                for p, vec_tiles, turned in waiting:
-                    for i, vec_tile in enumerate(vec_tiles):
-                        add_turned(nc, ident_f32, turned, vec_tile, first=False, last=(i == len(vec_tiles) - 1))
+                for p, max_sum, turned in waiting:
+                    add_turned(nc, ident_f32, turned, max_sum, first=False, last=True)
                 current = []
                 if pair < N_PAIR:
                     for p in (2 * pair, 2 * pair + 1):
+                        max_sum = sum_pool.tile([P, B], F32)
                         turned = bank_pool.tile([P, N_BT, P], F32, tag="bank")
-                        current.append((p, [], turned))
-                    for i in range(N_ACT):
-                        for p, vec_tiles, turned in current:
+                        current.append((p, max_sum, turned))
+                    for step in range(N_ACT):
+                        for p, max_sum, turned in current:
                             half_abs = act_pool.tile([P, B], F32)
                             nc.scalar.activation(
                                 out=half_abs[:],
-                                in_=feat_t[:, N_VEC + i, :],
+                                in_=feat_t[:, N_VEC + step, :],
                                 func=ACT.Abs,
-                                bias=proto_act_half[:, i, p : p + 1],
+                                bias=proto_act_half[:, step, p : p + 1],
                                 scale=-0.5,
                             )
-                            add_turned(nc, ident_f32, turned, half_abs, first=(i == 0), last=False)
-                    for p, vec_tiles, turned in current:
-                        max_sum = vec_pool.tile([P, B], F32)
-                        nc.vector.tensor_scalar(
-                            out=max_sum[:],
-                            in0=feat_t[:, 0, :],
-                            scalar1=proto_vec[:, 0, p : p + 1],
-                            scalar2=proto_neg_half_sum[:, p : p + 1],
-                            op0=ALU.max,
-                            op1=ALU.add,
+                            add_turned(nc, ident_f32, turned, half_abs, first=(step == 0), last=False)
+                        if step < N_ALONE:
+                            for p, max_sum, turned in current:
+                                max_alone = alone_pool.tile([P, B], F32)
+                                nc.vector.tensor_scalar(
+                                    out=max_alone[:],
+                                    in0=feat_t[:, N_CHAIN + step, :],
+                                    scalar1=proto_vec[:, N_CHAIN + step, p : p + 1],
+                                    scalar2=None,
+                                    op0=ALU.max,
+                                )
+                                add_turned(nc, ident_f32, turned, max_alone, first=False, last=False)
+                        if step == 0:
+                            for p, max_sum, turned in current:
+                                nc.vector.tensor_scalar(
+                                    out=max_sum[:],
+                                    in0=feat_t[:, 0, :],
+                                    scalar1=proto_vec[:, 0, p : p + 1],
+                                    scalar2=proto_neg_half_sum[:, p : p + 1],
+                                    op0=ALU.max,
+                                    op1=ALU.add,
+                                )
+                        elif step < N_CHAIN:
+                            for p, max_sum, turned in current:
+                                nc.vector.scalar_tensor_tensor(
+                                    out=max_sum[:],
+                                    in0=feat_t[:, step, :],
+                                    scalar=proto_vec[:, step, p : p + 1],
+                                    in1=max_sum[:],
+                                    op0=ALU.max,
+                                    op1=ALU.add,
+                                )
+                for p, max_sum, turned in waiting:
+                    for bt in range(N_BT):
+                        dropped = drop_pool.tile([P, P], F32)
+                        nc.scalar.activation(
+                            out=dropped[:], in_=turned[:, bt, :], func=ACT.Identity, accum_out=half_sum[:, p, bt : bt + 1]
                         )
-                        vec_tiles.append(max_sum)
-                    for c in range(1, N_CHAIN):
-                        for p, vec_tiles, turned in current:
-                            nc.vector.scalar_tensor_tensor(
-                                out=vec_tiles[0][:],
-                                in0=feat_t[:, c, :],
-                                scalar=proto_vec[:, c, p : p + 1],
-                                in1=vec_tiles[0][:],
-                                op0=ALU.max,
-                                op1=ALU.add,
-                            )
-                    for c in range(N_CHAIN, N_VEC):
-                        for p, vec_tiles, turned in current:
-                            max_alone = vec_pool.tile([P, B], F32)
-                            nc.vector.tensor_scalar(
-                                out=max_alone[:],
-                                in0=feat_t[:, c, :],
-                                scalar1=proto_vec[:, c, p : p + 1],
-                                scalar2=None,
-                                op0=ALU.max,
-                            )
-                            vec_tiles.append(max_alone)
-                for p, vec_tiles, turned in waiting:
-                    nc.vector.tensor_reduce(out=half_sum[:, p, :], in_=turned[:], axis=AXIS.X, op=ALU.add)
                 waiting = current
 
         result = small.tile([P, N_BT, N_PROTO], F32)

@@ -22,10 +22,10 @@ BANK = 512
 B, D, F0, F1, N_PROTO = 512, 2048, 1024, 512, 200
 N_BT = B // P
 N_CHUNK = D // P
-N_CHAIN = 5
-N_ALONE = 5
-N_VEC = N_CHAIN + N_ALONE
+N_VEC = 10
 N_ACT = N_CHUNK - N_VEC
+N_CHAIN_EVEN = 5
+N_CHAIN_ODD = 6
 N_PAIR = N_PROTO // 2
 
 FLOPS = 2 * B * (D * D + F1 * F0 + F0 * D) + 3 * B * N_PROTO * D
@@ -68,7 +68,7 @@ def group_computed_rows(nc, turn_psum, ident_bf16, rows, k0, grouped):
         )
 
 
-def build_features(tc, ins, ident_f32, feat_t, proto_vec, proto_act_half, proto_neg_half_sum):
+def build_features(tc, ins, ident_f32, feat_t, feat_sum, proto_vec, proto_act_half, proto_neg_half_sum):
     nc = tc.nc
     (x, aw_words, aw_scales, ab, h_up, h_skip, wu2_words, wu2_scales, bu2, wu3_words, wu3_scales, bu3, protos) = ins
     with ExitStack() as ctx:
@@ -86,35 +86,35 @@ def build_features(tc, ins, ident_f32, feat_t, proto_vec, proto_act_half, proto_
         zero(nc, wu2_s[:])
         zero(nc, aw_s[:])
         zero(nc, wu3_s[:])
-        load_scale_rows(nc, wu2_s, wu2_scales)
-        load_scale_rows(nc, aw_s, aw_scales)
-        load_scale_rows(nc, wu3_s, wu3_scales)
-
         h_up_sb = res.tile([P, N_BT, F1], BF16)
         h_skip_sb = res.tile([P, N_BT, F1], BF16)
         nc.sync.dma_start(out=h_up_sb[:], in_=h_up.rearrange("(t b) k -> b t k", b=P))
         nc.sync.dma_start(out=h_skip_sb[:], in_=h_skip.rearrange("(t b) k -> b t k", b=P))
+        load_scale_rows(nc, wu2_s, wu2_scales)
         wu2_w = res.tile([P, 2 * F0], U8, align_bytes=64)
         load_bytes(nc, wu2_w[:], wu2_words[0])
-        x_sb = res.tile([P, N_BT, D], BF16)
-        for bt in range(N_BT):
-            nc.sync.dma_start(out=x_sb[:, bt, :], in_=x[P * bt : P * (bt + 1), :])
-        bu2_all = res.tile([P, F0], BF16)
-        nc.sync.dma_start(out=bu2_all[:], in_=bu2.partition_broadcast(P))
-        bias_rows = res.tile([P, P], BF16)
-        zero(nc, bias_rows[:])
-        nc.sync.dma_start(out=bias_rows[0:N_CHUNK, :], in_=ab.rearrange("(c m) -> c m", m=P))
-        nc.sync.dma_start(out=bias_rows[N_CHUNK : 2 * N_CHUNK, :], in_=bu3.rearrange("(c m) -> c m", m=P))
+        load_scale_rows(nc, aw_s, aw_scales)
         aw_w = res.tile([P, D // K_PASS, 2 * D], U8, align_bytes=64)
         for g in range(D // K_PASS):
             load_bytes(nc, aw_w[:, g, :], aw_words[g])
+        load_scale_rows(nc, wu3_s, wu3_scales)
         wu3_w = res.tile([P, F0 // K_PASS, 2 * D], U8, align_bytes=64)
         for g in range(F0 // K_PASS):
             load_bytes(nc, wu3_w[:, g, :], wu3_words[g])
+
+        x_sb = res.tile([P, N_BT, D], BF16)
+        for bt in range(N_BT):
+            nc.scalar.dma_start(out=x_sb[:, bt, :], in_=x[P * bt : P * (bt + 1), :])
+        bu2_all = res.tile([P, F0], BF16)
+        nc.scalar.dma_start(out=bu2_all[:], in_=bu2.partition_broadcast(P))
+        bias_rows = res.tile([P, P], BF16)
+        zero(nc, bias_rows[:])
+        nc.scalar.dma_start(out=bias_rows[0:N_CHUNK, :], in_=ab.rearrange("(c m) -> c m", m=P))
+        nc.scalar.dma_start(out=bias_rows[N_CHUNK : 2 * N_CHUNK, :], in_=bu3.rearrange("(c m) -> c m", m=P))
         protos_sb = res.tile([P, 2, D], BF16)
         zero(nc, protos_sb[:, 1, :])
-        nc.sync.dma_start(out=protos_sb[:, 0, :], in_=protos[0:P, :])
-        nc.sync.dma_start(out=protos_sb[0 : N_PROTO - P, 1, :], in_=protos[P:N_PROTO, :])
+        nc.scalar.dma_start(out=protos_sb[:, 0, :], in_=protos[0:P, :])
+        nc.scalar.dma_start(out=protos_sb[0 : N_PROTO - P, 1, :], in_=protos[P:N_PROTO, :])
 
         z_sb = res.tile([P, N_BT, F1], BF16)
         nc.vector.tensor_tensor(out=z_sb[:], in0=h_up_sb[:], in1=h_skip_sb[:], op=ALU.add)
@@ -233,6 +233,10 @@ def build_features(tc, ins, ident_f32, feat_t, proto_vec, proto_act_half, proto_
                 out=u3[:], in_=u3_ps[:], func=ACT.Relu, bias=bias_cols[:, N_CHUNK + c : N_CHUNK + c + 1], scale=1.0
             )
             nc.vector.tensor_tensor(out=feat_t[:, c, :], in0=u3[:], in1=feat_t[:, c, :], op=ALU.add)
+            if c == 1:
+                nc.vector.tensor_tensor(out=feat_sum[:], in0=feat_t[:, 0, :], in1=feat_t[:, 1, :], op=ALU.add)
+            elif 1 < c < N_VEC:
+                nc.vector.tensor_tensor(out=feat_sum[:], in0=feat_t[:, c, :], in1=feat_sum[:], op=ALU.add)
 
 
 def add_turned(nc, ident_f32, turned, block_row, first, last):
@@ -247,7 +251,7 @@ def add_turned(nc, ident_f32, turned, block_row, first, last):
         )
 
 
-def sum_distances(tc, ident_f32, feat_t, proto_vec, proto_act_half, proto_neg_half_sum, out):
+def sum_distances(tc, ident_f32, feat_t, feat_sum, proto_vec, proto_act_half, proto_neg_half_sum, out):
     nc = tc.nc
     with ExitStack() as ctx:
         small = ctx.enter_context(tc.tile_pool(name="small", bufs=1))
@@ -259,28 +263,22 @@ def sum_distances(tc, ident_f32, feat_t, proto_vec, proto_act_half, proto_neg_ha
 
         half_sum = small.tile([P, N_PROTO, N_BT], F32)
 
-        feat_sum = small.tile([P, B], F32)
-        nc.vector.tensor_reduce(
-            out=feat_sum[:], in_=feat_t[:, 0:N_VEC, :].rearrange("m c b -> m b c"), axis=AXIS.X, op=ALU.add
-        )
-        feat_turned = bank_pool.tile([P, N_BT, P], F32, tag="bank")
+        feat_turned = bank_pool.tile([P, N_BT, P], F32, tag="feat_bank", bufs=1)
         add_turned(nc, ident_f32, feat_turned, feat_sum, first=True, last=True)
-        feat_rowsum = small.tile([P, N_BT], F32)
-        nc.vector.tensor_reduce(out=feat_rowsum[:], in_=feat_turned[:], axis=AXIS.X, op=ALU.add)
 
         with tc.manual_schedule():
             waiting = []
             for pair in range(N_PAIR + 1):
-                for p, max_sum, turned in waiting:
+                for p, n_chain, max_sum, turned in waiting:
                     add_turned(nc, ident_f32, turned, max_sum, first=False, last=True)
                 current = []
                 if pair < N_PAIR:
-                    for p in (2 * pair, 2 * pair + 1):
+                    for p, n_chain in ((2 * pair, N_CHAIN_EVEN), (2 * pair + 1, N_CHAIN_ODD)):
                         max_sum = sum_pool.tile([P, B], F32)
                         turned = bank_pool.tile([P, N_BT, P], F32, tag="bank")
-                        current.append((p, max_sum, turned))
+                        current.append((p, n_chain, max_sum, turned))
                     for step in range(N_ACT):
-                        for p, max_sum, turned in current:
+                        for p, n_chain, max_sum, turned in current:
                             half_abs = act_pool.tile([P, B], F32)
                             nc.scalar.activation(
                                 out=half_abs[:],
@@ -290,19 +288,20 @@ def sum_distances(tc, ident_f32, feat_t, proto_vec, proto_act_half, proto_neg_ha
                                 scale=-0.5,
                             )
                             add_turned(nc, ident_f32, turned, half_abs, first=(step == 0), last=False)
-                        if step < N_ALONE:
-                            for p, max_sum, turned in current:
+                        c_alone = N_VEC - 1 - step
+                        for p, n_chain, max_sum, turned in current:
+                            if c_alone >= n_chain:
                                 max_alone = alone_pool.tile([P, B], F32)
                                 nc.vector.tensor_scalar(
                                     out=max_alone[:],
-                                    in0=feat_t[:, N_CHAIN + step, :],
-                                    scalar1=proto_vec[:, N_CHAIN + step, p : p + 1],
+                                    in0=feat_t[:, c_alone, :],
+                                    scalar1=proto_vec[:, c_alone, p : p + 1],
                                     scalar2=None,
                                     op0=ALU.max,
                                 )
                                 add_turned(nc, ident_f32, turned, max_alone, first=False, last=False)
-                        if step == 0:
-                            for p, max_sum, turned in current:
+                        for p, n_chain, max_sum, turned in reversed(current):
+                            if step == 0:
                                 nc.vector.tensor_scalar(
                                     out=max_sum[:],
                                     in0=feat_t[:, 0, :],
@@ -311,8 +310,7 @@ def sum_distances(tc, ident_f32, feat_t, proto_vec, proto_act_half, proto_neg_ha
                                     op0=ALU.max,
                                     op1=ALU.add,
                                 )
-                        elif step < N_CHAIN:
-                            for p, max_sum, turned in current:
+                            elif step < n_chain:
                                 nc.vector.scalar_tensor_tensor(
                                     out=max_sum[:],
                                     in0=feat_t[:, step, :],
@@ -321,7 +319,7 @@ def sum_distances(tc, ident_f32, feat_t, proto_vec, proto_act_half, proto_neg_ha
                                     op0=ALU.max,
                                     op1=ALU.add,
                                 )
-                for p, max_sum, turned in waiting:
+                for p, n_chain, max_sum, turned in waiting:
                     for bt in range(N_BT):
                         dropped = drop_pool.tile([P, P], F32)
                         nc.scalar.activation(
@@ -329,6 +327,8 @@ def sum_distances(tc, ident_f32, feat_t, proto_vec, proto_act_half, proto_neg_ha
                         )
                 waiting = current
 
+        feat_rowsum = small.tile([P, N_BT], F32)
+        nc.vector.tensor_reduce(out=feat_rowsum[:], in_=feat_turned[:], axis=AXIS.X, op=ALU.add)
         result = small.tile([P, N_BT, N_PROTO], F32)
         for bt in range(N_BT):
             nc.vector.tensor_scalar(
@@ -350,9 +350,10 @@ def tile_prototypelearnerv4_pa_kernel(
         ident_f32 = keep.tile([P, P], F32)
         make_identity(nc, ident_f32[:])
         feat_t = keep.tile([P, N_CHUNK, B], F32)
+        feat_sum = keep.tile([P, B], F32)
         proto_vec = keep.tile([P, N_VEC, N_PROTO], F32)
         proto_act_half = keep.tile([P, N_ACT, N_PROTO], F32)
         proto_neg_half_sum = keep.tile([P, N_PROTO], F32)
         ins = (x, aW_words, aW_scales, ab, h_up, h_skip, Wu2_words, Wu2_scales, bu2, Wu3_words, Wu3_scales, bu3, protos)
-        build_features(tc, ins, ident_f32, feat_t, proto_vec, proto_act_half, proto_neg_half_sum)
-        sum_distances(tc, ident_f32, feat_t, proto_vec, proto_act_half, proto_neg_half_sum, out)
+        build_features(tc, ins, ident_f32, feat_t, feat_sum, proto_vec, proto_act_half, proto_neg_half_sum)
+        sum_distances(tc, ident_f32, feat_t, feat_sum, proto_vec, proto_act_half, proto_neg_half_sum, out)

@@ -22,10 +22,10 @@ BANK = 512
 B, D, F0, F1, N_PROTO = 512, 2048, 1024, 512, 200
 N_BT = B // P
 N_CHUNK = D // P
-N_VEC = 10
+N_CHAIN = 4
+N_ALONE = 5
+N_VEC = N_CHAIN + N_ALONE
 N_ACT = N_CHUNK - N_VEC
-N_CHAIN_EVEN = 5
-N_CHAIN_ODD = 6
 N_PAIR = N_PROTO // 2
 
 FLOPS = 2 * B * (D * D + F1 * F0 + F0 * D) + 3 * B * N_PROTO * D
@@ -256,9 +256,8 @@ def sum_distances(tc, ident_f32, feat_t, feat_sum, proto_vec, proto_act_half, pr
     with ExitStack() as ctx:
         small = ctx.enter_context(tc.tile_pool(name="small", bufs=1))
         act_pool = ctx.enter_context(tc.tile_pool(name="act_pool", bufs=8))
-        alone_pool = ctx.enter_context(tc.tile_pool(name="alone_pool", bufs=6))
+        alone_pool = ctx.enter_context(tc.tile_pool(name="alone_pool", bufs=4 * N_ALONE))
         sum_pool = ctx.enter_context(tc.tile_pool(name="sum_pool", bufs=4))
-        drop_pool = ctx.enter_context(tc.tile_pool(name="drop_pool", bufs=2))
         bank_pool = ctx.enter_context(tc.psum_pool(name="bank_pool", bufs=6))
 
         half_sum = small.tile([P, N_PROTO, N_BT], F32)
@@ -267,64 +266,64 @@ def sum_distances(tc, ident_f32, feat_t, feat_sum, proto_vec, proto_act_half, pr
         add_turned(nc, ident_f32, feat_turned, feat_sum, first=True, last=True)
 
         with tc.manual_schedule():
+            closed = []
             waiting = []
-            for pair in range(N_PAIR + 1):
-                for p, n_chain, max_sum, turned in waiting:
-                    add_turned(nc, ident_f32, turned, max_sum, first=False, last=True)
+            for pair in range(N_PAIR + 2):
                 current = []
                 if pair < N_PAIR:
-                    for p, n_chain in ((2 * pair, N_CHAIN_EVEN), (2 * pair + 1, N_CHAIN_ODD)):
+                    for p in (2 * pair, 2 * pair + 1):
                         max_sum = sum_pool.tile([P, B], F32)
                         turned = bank_pool.tile([P, N_BT, P], F32, tag="bank")
-                        current.append((p, n_chain, max_sum, turned))
-                    for step in range(N_ACT):
-                        for p, n_chain, max_sum, turned in current:
-                            half_abs = act_pool.tile([P, B], F32)
-                            nc.scalar.activation(
-                                out=half_abs[:],
-                                in_=feat_t[:, N_VEC + step, :],
-                                func=ACT.Abs,
-                                bias=proto_act_half[:, step, p : p + 1],
-                                scale=-0.5,
-                            )
-                            add_turned(nc, ident_f32, turned, half_abs, first=(step == 0), last=False)
-                        c_alone = N_VEC - 1 - step
-                        for p, n_chain, max_sum, turned in current:
-                            if c_alone >= n_chain:
-                                max_alone = alone_pool.tile([P, B], F32)
-                                nc.vector.tensor_scalar(
-                                    out=max_alone[:],
-                                    in0=feat_t[:, c_alone, :],
-                                    scalar1=proto_vec[:, c_alone, p : p + 1],
-                                    scalar2=None,
-                                    op0=ALU.max,
-                                )
-                                add_turned(nc, ident_f32, turned, max_alone, first=False, last=False)
-                        for p, n_chain, max_sum, turned in reversed(current):
-                            if step == 0:
-                                nc.vector.tensor_scalar(
-                                    out=max_sum[:],
-                                    in0=feat_t[:, 0, :],
-                                    scalar1=proto_vec[:, 0, p : p + 1],
-                                    scalar2=proto_neg_half_sum[:, p : p + 1],
-                                    op0=ALU.max,
-                                    op1=ALU.add,
-                                )
-                            elif step < n_chain:
-                                nc.vector.scalar_tensor_tensor(
-                                    out=max_sum[:],
-                                    in0=feat_t[:, step, :],
-                                    scalar=proto_vec[:, step, p : p + 1],
-                                    in1=max_sum[:],
-                                    op0=ALU.max,
-                                    op1=ALU.add,
-                                )
-                for p, n_chain, max_sum, turned in waiting:
-                    for bt in range(N_BT):
-                        dropped = drop_pool.tile([P, P], F32)
+                        current.append((p, [max_sum], turned))
+
+                for step in range(N_ACT):
+                    for p, vec_tiles, turned in current:
+                        half_abs = act_pool.tile([P, B], F32)
                         nc.scalar.activation(
-                            out=dropped[:], in_=turned[:, bt, :], func=ACT.Identity, accum_out=half_sum[:, p, bt : bt + 1]
+                            out=half_abs[:],
+                            in_=feat_t[:, N_VEC + step, :],
+                            func=ACT.Abs,
+                            bias=proto_act_half[:, step, p : p + 1],
+                            scale=-0.5,
                         )
+                        add_turned(nc, ident_f32, turned, half_abs, first=(step == 0), last=False)
+                    if step <= N_ALONE:
+                        for p, vec_tiles, turned in waiting:
+                            add_turned(nc, ident_f32, turned, vec_tiles[step], first=False, last=(step == N_ALONE))
+
+                for p, vec_tiles, turned in closed:
+                    nc.vector.tensor_reduce(out=half_sum[:, p, :], in_=turned[:], axis=AXIS.X, op=ALU.add)
+                for step in range(N_ALONE):
+                    for p, vec_tiles, turned in current:
+                        max_alone = alone_pool.tile([P, B], F32)
+                        nc.vector.tensor_scalar(
+                            out=max_alone[:],
+                            in0=feat_t[:, N_CHAIN + step, :],
+                            scalar1=proto_vec[:, N_CHAIN + step, p : p + 1],
+                            scalar2=None,
+                            op0=ALU.max,
+                        )
+                        vec_tiles.append(max_alone)
+                    for p, vec_tiles, turned in current:
+                        if step == 0:
+                            nc.vector.tensor_scalar(
+                                out=vec_tiles[0][:],
+                                in0=feat_t[:, 0, :],
+                                scalar1=proto_vec[:, 0, p : p + 1],
+                                scalar2=proto_neg_half_sum[:, p : p + 1],
+                                op0=ALU.max,
+                                op1=ALU.add,
+                            )
+                        elif step < N_CHAIN:
+                            nc.vector.scalar_tensor_tensor(
+                                out=vec_tiles[0][:],
+                                in0=feat_t[:, step, :],
+                                scalar=proto_vec[:, step, p : p + 1],
+                                in1=vec_tiles[0][:],
+                                op0=ALU.max,
+                                op1=ALU.add,
+                            )
+                closed = waiting
                 waiting = current
 
         feat_rowsum = small.tile([P, N_BT], F32)

@@ -27,6 +27,8 @@ N_ALONE = 5
 N_VEC = N_CHAIN + N_ALONE
 N_ACT = N_CHUNK - N_VEC
 N_PAIR = N_PROTO // 2
+PERIOD = 4
+N_SLOT = 3
 
 FLOPS = 2 * B * (D * D + F1 * F0 + F0 * D) + 3 * B * N_PROTO * D
 
@@ -258,6 +260,7 @@ def sum_distances(tc, ident_f32, feat_t, feat_sum, proto_vec, proto_act_half, pr
         act_pool = ctx.enter_context(tc.tile_pool(name="act_pool", bufs=8))
         alone_pool = ctx.enter_context(tc.tile_pool(name="alone_pool", bufs=4 * N_ALONE))
         sum_pool = ctx.enter_context(tc.tile_pool(name="sum_pool", bufs=4))
+        swap_pool = ctx.enter_context(tc.tile_pool(name="swap_pool", bufs=1))
         bank_pool = ctx.enter_context(tc.psum_pool(name="bank_pool", bufs=6))
 
         half_sum = small.tile([P, N_PROTO, N_BT], F32)
@@ -272,57 +275,92 @@ def sum_distances(tc, ident_f32, feat_t, feat_sum, proto_vec, proto_act_half, pr
                 current = []
                 if pair < N_PAIR:
                     for p in (2 * pair, 2 * pair + 1):
-                        max_sum = sum_pool.tile([P, B], F32)
                         turned = bank_pool.tile([P, N_BT, P], F32, tag="bank")
-                        current.append((p, [max_sum], turned))
+                        current.append((p, [], turned))
+                n_act = N_ACT if current else 0
+                n_turn = len(waiting[0][1]) if waiting else 0
 
-                for step in range(N_ACT):
-                    for p, vec_tiles, turned in current:
-                        half_abs = act_pool.tile([P, B], F32)
-                        nc.scalar.activation(
-                            out=half_abs[:],
-                            in_=feat_t[:, N_VEC + step, :],
-                            func=ACT.Abs,
-                            bias=proto_act_half[:, step, p : p + 1],
-                            scale=-0.5,
-                        )
-                        add_turned(nc, ident_f32, turned, half_abs, first=(step == 0), last=False)
-                    if step <= N_ALONE:
+                for step in range(max(n_act, n_turn)):
+                    if step < n_act:
+                        for p, vec_tiles, turned in current:
+                            half_abs = act_pool.tile([P, B], F32)
+                            nc.scalar.activation(
+                                out=half_abs[:],
+                                in_=feat_t[:, N_VEC + step, :],
+                                func=ACT.Abs,
+                                bias=proto_act_half[:, step, p : p + 1],
+                                scale=-0.5,
+                            )
+                            add_turned(nc, ident_f32, turned, half_abs, first=(step == 0), last=False)
+                    if step < n_turn:
                         for p, vec_tiles, turned in waiting:
-                            add_turned(nc, ident_f32, turned, vec_tiles[step], first=False, last=(step == N_ALONE))
+                            add_turned(nc, ident_f32, turned, vec_tiles[step], first=False, last=(step == n_turn - 1))
 
                 for p, vec_tiles, turned in closed:
                     nc.vector.tensor_reduce(out=half_sum[:, p, :], in_=turned[:], axis=AXIS.X, op=ALU.add)
-                for step in range(N_ALONE):
-                    for p, vec_tiles, turned in current:
-                        max_alone = alone_pool.tile([P, B], F32)
-                        nc.vector.tensor_scalar(
-                            out=max_alone[:],
-                            in0=feat_t[:, N_CHAIN + step, :],
-                            scalar1=proto_vec[:, N_CHAIN + step, p : p + 1],
-                            scalar2=None,
-                            op0=ALU.max,
-                        )
-                        vec_tiles.append(max_alone)
-                    for p, vec_tiles, turned in current:
-                        if step == 0:
-                            nc.vector.tensor_scalar(
-                                out=vec_tiles[0][:],
-                                in0=feat_t[:, 0, :],
-                                scalar1=proto_vec[:, 0, p : p + 1],
-                                scalar2=proto_neg_half_sum[:, p : p + 1],
-                                op0=ALU.max,
-                                op1=ALU.add,
-                            )
-                        elif step < N_CHAIN:
-                            nc.vector.scalar_tensor_tensor(
-                                out=vec_tiles[0][:],
-                                in0=feat_t[:, step, :],
-                                scalar=proto_vec[:, step, p : p + 1],
-                                in1=vec_tiles[0][:],
-                                op0=ALU.max,
-                                op1=ALU.add,
-                            )
+                if current:
+                    n_chain = N_CHAIN + 1 if pair % PERIOD == 0 else N_CHAIN
+                    n_plain = N_VEC - n_chain
+                    slot = pair % N_SLOT
+                    work_a = sum_pool.tile([P, B], F32, tag="work_a")
+                    work_b = swap_pool.tile([P, B], F32, tag="work_b%d" % slot, offset=slot * B * 4)
+                    work = [work_a, work_b]
+                    sum_a = sum_pool.tile([P, B], F32, tag="sum_a")
+                    sum_b = sum_pool.tile([P, B], F32, tag="sum_b")
+                    final = [sum_a, sum_b]
+                    plain = [[], []]
+                    order = []
+                    for back in range(max(n_chain, n_plain)):
+                        if back < n_chain:
+                            order.append(("chain", n_chain - 1 - back))
+                        if back < n_plain:
+                            order.append(("plain", n_plain - 1 - back))
+                    for what, n in reversed(order):
+                        for i in range(2):
+                            p = current[i][0]
+                            if what == "plain" and i == 0 and n == n_plain - 1:
+                                pass
+                            elif what == "plain":
+                                max_alone = alone_pool.tile([P, B], F32)
+                                nc.vector.tensor_scalar(
+                                    out=max_alone[:],
+                                    in0=feat_t[:, n_chain + n, :],
+                                    scalar1=proto_vec[:, n_chain + n, p : p + 1],
+                                    scalar2=None,
+                                    op0=ALU.max,
+                                )
+                                plain[i].append(max_alone)
+                            elif n == 0:
+                                nc.vector.tensor_scalar(
+                                    out=work[i][:],
+                                    in0=feat_t[:, 0, :],
+                                    scalar1=proto_vec[:, 0, p : p + 1],
+                                    scalar2=proto_neg_half_sum[:, p : p + 1],
+                                    op0=ALU.max,
+                                    op1=ALU.add,
+                                )
+                            else:
+                                target = final[i] if n == n_chain - 1 else work[i]
+                                nc.vector.scalar_tensor_tensor(
+                                    out=target[:],
+                                    in0=feat_t[:, n, :],
+                                    scalar=proto_vec[:, n, p : p + 1],
+                                    in1=work[i][:],
+                                    op0=ALU.max,
+                                    op1=ALU.add,
+                                )
+                    max_pool = swap_pool.tile([P, B], F32, tag="max_pool%d" % slot, offset=slot * B * 4)
+                    nc.gpsimd.tensor_scalar(
+                        out=max_pool[:],
+                        in0=feat_t[:, N_VEC - 1, :],
+                        scalar1=proto_vec[:, N_VEC - 1, current[0][0] : current[0][0] + 1],
+                        scalar2=0.0,
+                        op0=ALU.max,
+                        op1=ALU.add,
+                    )
+                    plain[0].append(max_pool)
+                    for i in range(2):
+                        current[i][1].extend([final[i]] + plain[i])
                 closed = waiting
                 waiting = current
 

@@ -27,6 +27,7 @@ N_ALONE = 5
 N_VEC = N_CHAIN + N_ALONE
 N_ACT = N_CHUNK - N_VEC
 N_PAIR = N_PROTO // 2
+CHUNK_ORDER = tuple(range(N_VEC, N_CHUNK)) + tuple(range(N_VEC))
 PERIOD = 4
 N_SLOT = 3
 
@@ -54,30 +55,31 @@ def quantise(nc, codes, plane, grouped_bf16):
     nc.vector.quantize_mx(out=codes.bitcast(FP8X4), scales=plane, in_=grouped_bf16)
 
 
-def group_computed_rows(nc, turn_psum, ident_bf16, rows, k0, grouped):
+def group_rows(nc, turn_psum, ident_f32, rows, g, grouped, copies):
     for half in range(2):
-        turned = turn_psum.tile([P, PACK, 2 * P], BF16, tag="turn")
-        for t in range(PACK):
+        turned = turn_psum.tile([P, 2, 2 * P], F32, tag="turn", bufs=3)
+        for u in range(2):
             for i in range(2):
+                words = rows[:, 2 * half + i, :].bitcast(F32)
                 nc.tensor.transpose(
-                    turned[:, t, P * i : P * (i + 1)],
-                    rows[:, 2 * half + i, k0 + t : k0 + K_PASS : PACK],
-                    ident_bf16[:],
+                    turned[:, u, P * i : P * (i + 1)],
+                    words[:, 256 * g + u : 256 * (g + 1) : 2],
+                    ident_f32[:],
                 )
-        nc.vector.tensor_copy(
+        copies[half](
             out=grouped[:, 2 * P * half : 2 * P * (half + 1), :],
-            in_=turned[:].rearrange("p t b -> p b t"),
+            in_=turned[:].rearrange("p u b -> p b u"),
         )
 
 
-def build_features(tc, ins, ident_f32, feat_t, feat_sum, proto_vec, proto_act_half, proto_neg_half_sum):
+def build_features(tc, psum, ins, ident_f32, feat_t, feat_sum, proto_vec, proto_act_half, proto_neg_half_sum):
     nc = tc.nc
     (x, aw_words, aw_scales, ab, h_up, h_skip, wu2_words, wu2_scales, bu2, wu3_words, wu3_scales, bu3, protos) = ins
     with ExitStack() as ctx:
         res = ctx.enter_context(tc.tile_pool(name="resident", bufs=1))
         stage = ctx.enter_context(tc.tile_pool(name="stage", bufs=2))
-        turn_psum = ctx.enter_context(tc.psum_pool(name="turn_psum", bufs=3))
-        mm_psum = ctx.enter_context(tc.psum_pool(name="mm_psum", bufs=4))
+        turn_psum = psum
+        mm_psum = psum
 
         ident_bf16 = res.tile([P, P], BF16)
         make_identity(nc, ident_bf16[:])
@@ -91,7 +93,7 @@ def build_features(tc, ins, ident_f32, feat_t, feat_sum, proto_vec, proto_act_ha
         h_up_sb = res.tile([P, N_BT, F1], BF16)
         h_skip_sb = res.tile([P, N_BT, F1], BF16)
         nc.sync.dma_start(out=h_up_sb[:], in_=h_up.rearrange("(t b) k -> b t k", b=P))
-        nc.sync.dma_start(out=h_skip_sb[:], in_=h_skip.rearrange("(t b) k -> b t k", b=P))
+        nc.scalar.dma_start(out=h_skip_sb[:], in_=h_skip.rearrange("(t b) k -> b t k", b=P))
         load_scale_rows(nc, wu2_s, wu2_scales)
         wu2_w = res.tile([P, 2 * F0], U8, align_bytes=64)
         load_bytes(nc, wu2_w[:], wu2_words[0])
@@ -120,39 +122,26 @@ def build_features(tc, ins, ident_f32, feat_t, feat_sum, proto_vec, proto_act_ha
 
         z_sb = res.tile([P, N_BT, F1], BF16)
         nc.vector.tensor_tensor(out=z_sb[:], in0=h_up_sb[:], in1=h_skip_sb[:], op=ALU.add)
-        z_grouped = res.tile([P, B, PACK], BF16, align_bytes=64)
-        group_computed_rows(nc, turn_psum, ident_bf16, z_sb, 0, z_grouped)
+        z_grouped = res.tile([P, B, 2], F32, align_bytes=64)
+        group_rows(nc, turn_psum, ident_f32, z_sb, 0, z_grouped, (nc.vector.tensor_copy, nc.vector.tensor_copy))
         z_codes = res.tile([P, B], U32, align_bytes=64)
         z_plane = res.tile([P, B], U8, align_bytes=64)
-        quantise(nc, z_codes[:], z_plane[:], z_grouped[:].rearrange("p b t -> p (b t)"))
+        quantise(nc, z_codes[:], z_plane[:], z_grouped[:].rearrange("p b u -> p (b u)").bitcast(BF16))
 
         x_codes = res.tile([P, D // K_PASS, B], U32, align_bytes=64)
         x_plane = res.tile([P, D // K_PASS, B], U8, align_bytes=64)
         for g in range(D // K_PASS):
             x_grouped = stage.tile([P, B, 2], F32, align_bytes=64)
-            for half in range(2):
-                turned = turn_psum.tile([P, 2, 2 * P], F32, tag="turn")
-                for u in range(2):
-                    for i in range(2):
-                        x_words = x_sb[:, 2 * half + i, :].bitcast(F32)
-                        nc.tensor.transpose(
-                            turned[:, u, P * i : P * (i + 1)],
-                            x_words[:, 256 * g + u : 256 * (g + 1) : 2],
-                            ident_f32[:],
-                        )
-                nc.scalar.copy(
-                    out=x_grouped[:, 2 * P * half : 2 * P * (half + 1), :],
-                    in_=turned[:].rearrange("p u b -> p b u"),
-                )
+            group_rows(nc, turn_psum, ident_f32, x_sb, g, x_grouped, (nc.scalar.copy, nc.scalar.copy))
             quantise(
                 nc, x_codes[:, g, :], x_plane[:, g, :], x_grouped[:].rearrange("p b u -> p (b u)").bitcast(BF16)
             )
 
         u2_sb = res.tile([P, N_BT, F0], BF16)
-        for bt in range(N_BT):
-            for g in range(F0 // BANK):
+        for g in range(F0 // BANK):
+            for bt in range(N_BT):
                 n_cols = slice(BANK * g, BANK * (g + 1))
-                u2_ps = mm_psum.tile([P, BANK], F32, tag="mm")
+                u2_ps = mm_psum.tile([P, BANK], F32, tag="mm", bufs=4)
                 nc.tensor.matmul_mx(
                     out=u2_ps[:],
                     lhsT=z_codes[:, P * bt : P * (bt + 1)].bitcast(FP8X4),
@@ -166,46 +155,52 @@ def build_features(tc, ins, ident_f32, feat_t, feat_sum, proto_vec, proto_act_ha
                 nc.vector.tensor_tensor(out=u2_biased[:], in0=u2_ps[:], in1=bu2_all[:, n_cols], op=ALU.add)
                 nc.scalar.activation(out=u2_sb[:, bt, n_cols], in_=u2_biased[:], func=ACT.Relu)
 
-        bias_ps = turn_psum.tile([P, P], BF16, tag="turn")
+        u2_codes = res.tile([P, F0 // K_PASS, B], U32, align_bytes=64)
+        u2_plane = res.tile([P, F0 // K_PASS, B], U8, align_bytes=64)
+        for g in range(F0 // K_PASS):
+            u2_grouped = stage.tile([P, B, 2], F32, align_bytes=64)
+            group_rows(nc, turn_psum, ident_f32, u2_sb, g, u2_grouped, (nc.vector.tensor_copy, nc.scalar.copy))
+            quantise(
+                nc, u2_codes[:, g, :], u2_plane[:, g, :], u2_grouped[:].rearrange("p b u -> p (b u)").bitcast(BF16)
+            )
+
+        bias_ps = turn_psum.tile([P, P], BF16, tag="turn", bufs=3)
         nc.tensor.transpose(bias_ps[:], bias_rows[:], ident_bf16[:])
         bias_cols = res.tile([P, 2 * N_CHUNK], F32)
         nc.vector.tensor_copy(out=bias_cols[:], in_=bias_ps[:, 0 : 2 * N_CHUNK])
 
-        for c in range(N_CHUNK):
-            xt_ps = turn_psum.tile([P, B], BF16, tag="turn")
+        for c in CHUNK_ORDER:
+            xt_ps = turn_psum.tile([P, B], BF16, tag="turn", bufs=3)
             for bt in range(N_BT):
                 nc.tensor.transpose(xt_ps[:, P * bt : P * (bt + 1)], x_sb[:, bt, P * c : P * (c + 1)], ident_bf16[:])
             nc.scalar.activation(
                 out=feat_t[:, c, :], in_=xt_ps[:], func=ACT.Identity, bias=bias_cols[:, c : c + 1], scale=1.0
             )
 
+        proto_sum = res.tile([P, N_PROTO], F32)
         for c in range(N_CHUNK):
-            pt_ps = turn_psum.tile([P, 2 * P], BF16, tag="turn")
+            pt_ps = turn_psum.tile([P, 2 * P], BF16, tag="turn", bufs=3)
             for h in range(2):
                 nc.tensor.transpose(pt_ps[:, P * h : P * (h + 1)], protos_sb[:, h, P * c : P * (c + 1)], ident_bf16[:])
             if c < N_VEC:
                 nc.vector.tensor_copy(out=proto_vec[:, c, :], in_=pt_ps[:, 0:N_PROTO])
+                if c > 0:
+                    nc.vector.tensor_tensor(
+                        out=proto_sum[:],
+                        in0=pt_ps[:, 0:N_PROTO],
+                        in1=(proto_vec[:, 0, :] if c == 1 else proto_sum[:]),
+                        op=ALU.add,
+                    )
             else:
                 nc.vector.tensor_scalar(
                     out=proto_act_half[:, c - N_VEC, :], in0=pt_ps[:, 0:N_PROTO], scalar1=0.5, scalar2=None, op0=ALU.mult
                 )
-        proto_sum = res.tile([P, N_PROTO], F32)
-        nc.vector.tensor_reduce(
-            out=proto_sum[:], in_=proto_vec[:].rearrange("m c p -> m p c"), axis=AXIS.X, op=ALU.add
-        )
         nc.vector.tensor_scalar(
             out=proto_neg_half_sum[:], in0=proto_sum[:], scalar1=-0.5, scalar2=None, op0=ALU.mult
         )
 
-        u2_codes = res.tile([P, F0 // K_PASS, B], U32, align_bytes=64)
-        u2_plane = res.tile([P, F0 // K_PASS, B], U8, align_bytes=64)
-        for g in range(F0 // K_PASS):
-            u2_grouped = stage.tile([P, B, PACK], BF16, align_bytes=64)
-            group_computed_rows(nc, turn_psum, ident_bf16, u2_sb, K_PASS * g, u2_grouped)
-            quantise(nc, u2_codes[:, g, :], u2_plane[:, g, :], u2_grouped[:].rearrange("p b t -> p (b t)"))
-
-        for c in range(N_CHUNK):
-            a_ps = mm_psum.tile([P, B], F32, tag="mm")
+        for c in CHUNK_ORDER:
+            a_ps = mm_psum.tile([P, B], F32, tag="mm", bufs=4)
             for g in range(D // K_PASS):
                 nc.tensor.matmul_mx(
                     out=a_ps[:],
@@ -217,9 +212,7 @@ def build_features(tc, ins, ident_f32, feat_t, feat_sum, proto_vec, proto_act_ha
                     stop=(g == D // K_PASS - 1),
                 )
             nc.vector.tensor_tensor(out=feat_t[:, c, :], in0=a_ps[:], in1=feat_t[:, c, :], op=ALU.add)
-
-        for c in range(N_CHUNK):
-            u3_ps = mm_psum.tile([P, B], F32, tag="mm")
+            u3_ps = mm_psum.tile([P, B], F32, tag="mm", bufs=4)
             for g in range(F0 // K_PASS):
                 nc.tensor.matmul_mx(
                     out=u3_ps[:],
@@ -253,20 +246,18 @@ def add_turned(nc, ident_f32, turned, block_row, first, last):
         )
 
 
-def sum_distances(tc, ident_f32, feat_t, feat_sum, proto_vec, proto_act_half, proto_neg_half_sum, out):
+def sum_distances(tc, psum, act_pool, ident_f32, feat_t, feat_sum, proto_vec, proto_act_half, proto_neg_half_sum, out):
     nc = tc.nc
     with ExitStack() as ctx:
         small = ctx.enter_context(tc.tile_pool(name="small", bufs=1))
-        act_pool = ctx.enter_context(tc.tile_pool(name="act_pool", bufs=8))
         alone_pool = ctx.enter_context(tc.tile_pool(name="alone_pool", bufs=4 * N_ALONE))
         sum_pool = ctx.enter_context(tc.tile_pool(name="sum_pool", bufs=4))
         swap_pool = ctx.enter_context(tc.tile_pool(name="swap_pool", bufs=1))
-        bank_pool = ctx.enter_context(tc.psum_pool(name="bank_pool", bufs=6))
+        bank_pool = psum
 
         half_sum = small.tile([P, N_PROTO, N_BT], F32)
 
         feat_turned = bank_pool.tile([P, N_BT, P], F32, tag="feat_bank", bufs=1)
-        add_turned(nc, ident_f32, feat_turned, feat_sum, first=True, last=True)
 
         with tc.manual_schedule():
             closed = []
@@ -275,7 +266,10 @@ def sum_distances(tc, ident_f32, feat_t, feat_sum, proto_vec, proto_act_half, pr
                 current = []
                 if pair < N_PAIR:
                     for p in (2 * pair, 2 * pair + 1):
-                        turned = bank_pool.tile([P, N_BT, P], F32, tag="bank")
+                        if pair % 3 == 0:
+                            turned = bank_pool.tile([P, N_BT, P], F32, tag="turn", bufs=3)
+                        else:
+                            turned = bank_pool.tile([P, N_BT, P], F32, tag="mm", bufs=4)
                         current.append((p, [], turned))
                 n_act = N_ACT if current else 0
                 n_turn = len(waiting[0][1]) if waiting else 0
@@ -295,6 +289,9 @@ def sum_distances(tc, ident_f32, feat_t, feat_sum, proto_vec, proto_act_half, pr
                     if step < n_turn:
                         for p, vec_tiles, turned in waiting:
                             add_turned(nc, ident_f32, turned, vec_tiles[step], first=False, last=(step == n_turn - 1))
+
+                if pair == 2:
+                    add_turned(nc, ident_f32, feat_turned, feat_sum, first=True, last=True)
 
                 for p, vec_tiles, turned in closed:
                     nc.vector.tensor_reduce(out=half_sum[:, p, :], in_=turned[:], axis=AXIS.X, op=ALU.add)
@@ -358,9 +355,9 @@ def sum_distances(tc, ident_f32, feat_t, feat_sum, proto_vec, proto_act_half, pr
                         op0=ALU.max,
                         op1=ALU.add,
                     )
-                    plain[0].append(max_pool)
                     for i in range(2):
-                        current[i][1].extend([final[i]] + plain[i])
+                        current[i][1].extend(plain[i] + [final[i]])
+                    current[0][1].append(max_pool)
                 closed = waiting
                 waiting = current
 
@@ -392,5 +389,6 @@ def tile_prototypelearnerv4_pa_kernel(
         proto_act_half = keep.tile([P, N_ACT, N_PROTO], F32)
         proto_neg_half_sum = keep.tile([P, N_PROTO], F32)
         ins = (x, aW_words, aW_scales, ab, h_up, h_skip, Wu2_words, Wu2_scales, bu2, Wu3_words, Wu3_scales, bu3, protos)
-        build_features(tc, ins, ident_f32, feat_t, feat_sum, proto_vec, proto_act_half, proto_neg_half_sum)
-        sum_distances(tc, ident_f32, feat_t, feat_sum, proto_vec, proto_act_half, proto_neg_half_sum, out)
+        with tc.psum_pool(name="psum", bufs=1) as psum, tc.tile_pool(name="act_pool", bufs=16) as act_pool:
+            build_features(tc, psum, ins, ident_f32, feat_t, feat_sum, proto_vec, proto_act_half, proto_neg_half_sum)
+            sum_distances(tc, psum, act_pool, ident_f32, feat_t, feat_sum, proto_vec, proto_act_half, proto_neg_half_sum, out)

from contextlib import ExitStack

import concourse.mybir as mybir
from concourse.masks import make_identity

F32 = mybir.dt.float32
BF16 = mybir.dt.bfloat16
I32 = mybir.dt.int32
U32 = mybir.dt.uint32
U8 = mybir.dt.uint8
FP8X4 = mybir.dt.float8_e4m3fn_x4
FP4X4 = mybir.dt.float4_e2m1fn_x4
ALU = mybir.AluOpType
ACT = mybir.ActivationFunctionType
AXIS = mybir.AxisListType

P = 128
PACK = 4
K_PASS = P * PACK
BANK = 512

B, D, F0, F1, N_PROTO = 512, 2048, 1024, 512, 200
N_BT = B // P
N_CHUNK = D // P
N_CHAIN = 4
N_ALONE = 5
N_VEC = N_CHAIN + N_ALONE
N_ACT = N_CHUNK - N_VEC
N_PAIR = N_PROTO // 2
CHUNK_ORDER = tuple(range(N_VEC, N_CHUNK)) + tuple(range(N_VEC))
PERIOD = 4
N_SLOT = 3

FLOPS = 2 * B * (D * D + F1 * F0 + F0 * D) + 3 * B * N_PROTO * D


def zero(nc, tile_ap):
    nc.vector.memset(tile_ap.bitcast(I32), 0)


def load_bytes(nc, tile_ap, dram_ap):
    nc.sync.dma_start(out=tile_ap.bitcast(I32), in_=dram_ap.bitcast(I32))


def load_scale_rows(nc, planes, scales):
    for quadrant in range(4):
        load_bytes(
            nc,
            planes[32 * quadrant : 32 * quadrant + 4, :, :],
            scales[:, 4 * quadrant : 4 * quadrant + 4, :].rearrange("g r n -> r g n"),
        )


def quantise(nc, codes, plane, grouped_bf16):
    nc.vector.quantize_mx(out=codes.bitcast(FP8X4), scales=plane, in_=grouped_bf16)


def group_rows(nc, turn_psum, ident_f32, rows, g, grouped, copies):
    for half in range(2):
        turned = turn_psum.tile([P, 2, 2 * P], F32, tag="turn", bufs=3)
        for u in range(2):
            for i in range(2):
                words = rows[:, 2 * half + i, :].bitcast(F32)
                nc.tensor.transpose(
                    turned[:, u, P * i : P * (i + 1)],
                    words[:, 256 * g + u : 256 * (g + 1) : 2],
                    ident_f32[:],
                )
        copies[half](
            out=grouped[:, 2 * P * half : 2 * P * (half + 1), :],
            in_=turned[:].rearrange("p u b -> p b u"),
        )


def build_features(tc, psum, ins, ident_f32, feat_t, feat_sum, proto_vec, proto_act_half, proto_neg_half_sum):
    nc = tc.nc
    (x, aw_words, aw_scales, ab, h_up, h_skip, wu2_words, wu2_scales, bu2, wu3_words, wu3_scales, bu3, protos) = ins
    with ExitStack() as ctx:
        res = ctx.enter_context(tc.tile_pool(name="resident", bufs=1))
        stage = ctx.enter_context(tc.tile_pool(name="stage", bufs=2))
        turn_psum = psum
        mm_psum = psum

        ident_bf16 = res.tile([P, P], BF16)
        make_identity(nc, ident_bf16[:])

        wu2_s = res.tile([P, F1 // K_PASS, F0], U8, align_bytes=64)
        aw_s = res.tile([P, D // K_PASS, D], U8, align_bytes=64)
        wu3_s = res.tile([P, F0 // K_PASS, D], U8, align_bytes=64)
        zero(nc, wu2_s[:])
        zero(nc, aw_s[:])
        zero(nc, wu3_s[:])
        h_up_sb = res.tile([P, N_BT, F1], BF16)
        h_skip_sb = res.tile([P, N_BT, F1], BF16)
        nc.sync.dma_start(out=h_up_sb[:], in_=h_up.rearrange("(t b) k -> b t k", b=P))
        nc.scalar.dma_start(out=h_skip_sb[:], in_=h_skip.rearrange("(t b) k -> b t k", b=P))
        load_scale_rows(nc, wu2_s, wu2_scales)
        wu2_w = res.tile([P, 2 * F0], U8, align_bytes=64)
        load_bytes(nc, wu2_w[:], wu2_words[0])
        load_scale_rows(nc, aw_s, aw_scales)
        aw_w = res.tile([P, D // K_PASS, 2 * D], U8, align_bytes=64)
        for g in range(D // K_PASS):
            load_bytes(nc, aw_w[:, g, :], aw_words[g])
        load_scale_rows(nc, wu3_s, wu3_scales)
        wu3_w = res.tile([P, F0 // K_PASS, 2 * D], U8, align_bytes=64)
        for g in range(F0 // K_PASS):
            load_bytes(nc, wu3_w[:, g, :], wu3_words[g])

        x_sb = res.tile([P, N_BT, D], BF16)
        for bt in range(N_BT):
            nc.scalar.dma_start(out=x_sb[:, bt, :], in_=x[P * bt : P * (bt + 1), :])
        bu2_all = res.tile([P, F0], BF16)
        nc.scalar.dma_start(out=bu2_all[:], in_=bu2.partition_broadcast(P))
        bias_rows = res.tile([P, P], BF16)
        zero(nc, bias_rows[:])
        nc.scalar.dma_start(out=bias_rows[0:N_CHUNK, :], in_=ab.rearrange("(c m) -> c m", m=P))
        nc.scalar.dma_start(out=bias_rows[N_CHUNK : 2 * N_CHUNK, :], in_=bu3.rearrange("(c m) -> c m", m=P))
        protos_sb = res.tile([P, 2, D], BF16)
        zero(nc, protos_sb[:, 1, :])
        nc.scalar.dma_start(out=protos_sb[:, 0, :], in_=protos[0:P, :])
        nc.scalar.dma_start(out=protos_sb[0 : N_PROTO - P, 1, :], in_=protos[P:N_PROTO, :])

        z_sb = res.tile([P, N_BT, F1], BF16)
        nc.vector.tensor_tensor(out=z_sb[:], in0=h_up_sb[:], in1=h_skip_sb[:], op=ALU.add)
        z_grouped = res.tile([P, B, 2], F32, align_bytes=64)
        group_rows(nc, turn_psum, ident_f32, z_sb, 0, z_grouped, (nc.vector.tensor_copy, nc.vector.tensor_copy))
        z_codes = res.tile([P, B], U32, align_bytes=64)
        z_plane = res.tile([P, B], U8, align_bytes=64)
        quantise(nc, z_codes[:], z_plane[:], z_grouped[:].rearrange("p b u -> p (b u)").bitcast(BF16))

        x_codes = res.tile([P, D // K_PASS, B], U32, align_bytes=64)
        x_plane = res.tile([P, D // K_PASS, B], U8, align_bytes=64)
        for g in range(D // K_PASS):
            x_grouped = stage.tile([P, B, 2], F32, align_bytes=64)
            group_rows(nc, turn_psum, ident_f32, x_sb, g, x_grouped, (nc.scalar.copy, nc.scalar.copy))
            quantise(
                nc, x_codes[:, g, :], x_plane[:, g, :], x_grouped[:].rearrange("p b u -> p (b u)").bitcast(BF16)
            )

        u2_sb = res.tile([P, N_BT, F0], BF16)
        for g in range(F0 // BANK):
            for bt in range(N_BT):
                n_cols = slice(BANK * g, BANK * (g + 1))
                u2_ps = mm_psum.tile([P, BANK], F32, tag="mm", bufs=4)
                nc.tensor.matmul_mx(
                    out=u2_ps[:],
                    lhsT=z_codes[:, P * bt : P * (bt + 1)].bitcast(FP8X4),
                    lhsT_scale=z_plane[:, P * bt : P * (bt + 1)],
                    rhs=wu2_w[:, 2 * BANK * g : 2 * BANK * (g + 1)].bitcast(FP4X4),
                    rhs_scale=wu2_s[:, 0, n_cols],
                    start=True,
                    stop=True,
                )
                u2_biased = stage.tile([P, BANK], F32)
                nc.vector.tensor_tensor(out=u2_biased[:], in0=u2_ps[:], in1=bu2_all[:, n_cols], op=ALU.add)
                nc.scalar.activation(out=u2_sb[:, bt, n_cols], in_=u2_biased[:], func=ACT.Relu)

        u2_codes = res.tile([P, F0 // K_PASS, B], U32, align_bytes=64)
        u2_plane = res.tile([P, F0 // K_PASS, B], U8, align_bytes=64)
        for g in range(F0 // K_PASS):
            u2_grouped = stage.tile([P, B, 2], F32, align_bytes=64)
            group_rows(nc, turn_psum, ident_f32, u2_sb, g, u2_grouped, (nc.vector.tensor_copy, nc.scalar.copy))
            quantise(
                nc, u2_codes[:, g, :], u2_plane[:, g, :], u2_grouped[:].rearrange("p b u -> p (b u)").bitcast(BF16)
            )

        bias_ps = turn_psum.tile([P, P], BF16, tag="turn", bufs=3)
        nc.tensor.transpose(bias_ps[:], bias_rows[:], ident_bf16[:])
        bias_cols = res.tile([P, 2 * N_CHUNK], F32)
        nc.vector.tensor_copy(out=bias_cols[:], in_=bias_ps[:, 0 : 2 * N_CHUNK])

        for c in CHUNK_ORDER:
            xt_ps = turn_psum.tile([P, B], BF16, tag="turn", bufs=3)
            for bt in range(N_BT):
                nc.tensor.transpose(xt_ps[:, P * bt : P * (bt + 1)], x_sb[:, bt, P * c : P * (c + 1)], ident_bf16[:])
            nc.scalar.activation(
                out=feat_t[:, c, :], in_=xt_ps[:], func=ACT.Identity, bias=bias_cols[:, c : c + 1], scale=1.0
            )

        proto_sum = res.tile([P, N_PROTO], F32)
        for c in range(N_CHUNK):
            pt_ps = turn_psum.tile([P, 2 * P], BF16, tag="turn", bufs=3)
            for h in range(2):
                nc.tensor.transpose(pt_ps[:, P * h : P * (h + 1)], protos_sb[:, h, P * c : P * (c + 1)], ident_bf16[:])
            if c < N_VEC:
                nc.vector.tensor_copy(out=proto_vec[:, c, :], in_=pt_ps[:, 0:N_PROTO])
                if c > 0:
                    nc.vector.tensor_tensor(
                        out=proto_sum[:],
                        in0=pt_ps[:, 0:N_PROTO],
                        in1=(proto_vec[:, 0, :] if c == 1 else proto_sum[:]),
                        op=ALU.add,
                    )
            else:
                nc.vector.tensor_scalar(
                    out=proto_act_half[:, c - N_VEC, :], in0=pt_ps[:, 0:N_PROTO], scalar1=0.5, scalar2=None, op0=ALU.mult
                )
        nc.vector.tensor_scalar(
            out=proto_neg_half_sum[:], in0=proto_sum[:], scalar1=-0.5, scalar2=None, op0=ALU.mult
        )

        for c in CHUNK_ORDER:
            a_ps = mm_psum.tile([P, B], F32, tag="mm", bufs=4)
            for g in range(D // K_PASS):
                nc.tensor.matmul_mx(
                    out=a_ps[:],
                    lhsT=aw_w[:, g, 2 * P * c : 2 * P * (c + 1)].bitcast(FP4X4),
                    lhsT_scale=aw_s[:, g, P * c : P * (c + 1)],
                    rhs=x_codes[:, g, :].bitcast(FP8X4),
                    rhs_scale=x_plane[:, g, :],
                    start=(g == 0),
                    stop=(g == D // K_PASS - 1),
                )
            nc.vector.tensor_tensor(out=feat_t[:, c, :], in0=a_ps[:], in1=feat_t[:, c, :], op=ALU.add)
            u3_ps = mm_psum.tile([P, B], F32, tag="mm", bufs=4)
            for g in range(F0 // K_PASS):
                nc.tensor.matmul_mx(
                    out=u3_ps[:],
                    lhsT=wu3_w[:, g, 2 * P * c : 2 * P * (c + 1)].bitcast(FP4X4),
                    lhsT_scale=wu3_s[:, g, P * c : P * (c + 1)],
                    rhs=u2_codes[:, g, :].bitcast(FP8X4),
                    rhs_scale=u2_plane[:, g, :],
                    start=(g == 0),
                    stop=(g == F0 // K_PASS - 1),
                )
            u3 = stage.tile([P, B], F32)
            nc.scalar.activation(
                out=u3[:], in_=u3_ps[:], func=ACT.Relu, bias=bias_cols[:, N_CHUNK + c : N_CHUNK + c + 1], scale=1.0
            )
            nc.vector.tensor_tensor(out=feat_t[:, c, :], in0=u3[:], in1=feat_t[:, c, :], op=ALU.add)
            if c == 1:
                nc.vector.tensor_tensor(out=feat_sum[:], in0=feat_t[:, 0, :], in1=feat_t[:, 1, :], op=ALU.add)
            elif 1 < c < N_VEC:
                nc.vector.tensor_tensor(out=feat_sum[:], in0=feat_t[:, c, :], in1=feat_sum[:], op=ALU.add)


def add_turned(nc, ident_f32, turned, block_row, first, last):
    for bt in range(N_BT):
        nc.tensor.matmul(
            out=turned[:, bt, :],
            lhsT=block_row[:, P * bt : P * (bt + 1)],
            rhs=ident_f32[:],
            is_transpose=True,
            start=(first and bt == 0),
            stop=(last and bt == N_BT - 1),
        )


def sum_distances(tc, psum, act_pool, ident_f32, feat_t, feat_sum, proto_vec, proto_act_half, proto_neg_half_sum, out):
    nc = tc.nc
    with ExitStack() as ctx:
        small = ctx.enter_context(tc.tile_pool(name="small", bufs=1))
        alone_pool = ctx.enter_context(tc.tile_pool(name="alone_pool", bufs=4 * N_ALONE))
        sum_pool = ctx.enter_context(tc.tile_pool(name="sum_pool", bufs=4))
        swap_pool = ctx.enter_context(tc.tile_pool(name="swap_pool", bufs=1))
        bank_pool = psum

        half_sum = small.tile([P, N_PROTO, N_BT], F32)

        feat_turned = bank_pool.tile([P, N_BT, P], F32, tag="feat_bank", bufs=1)

        with tc.manual_schedule():
            closed = []
            waiting = []
            for pair in range(N_PAIR + 2):
                current = []
                if pair < N_PAIR:
                    for p in (2 * pair, 2 * pair + 1):
                        if pair % 3 == 0:
                            turned = bank_pool.tile([P, N_BT, P], F32, tag="turn", bufs=3)
                        else:
                            turned = bank_pool.tile([P, N_BT, P], F32, tag="mm", bufs=4)
                        current.append((p, [], turned))
                n_act = N_ACT if current else 0
                n_turn = len(waiting[0][1]) if waiting else 0

                for step in range(max(n_act, n_turn)):
                    if step < n_act:
                        for p, vec_tiles, turned in current:
                            half_abs = act_pool.tile([P, B], F32)
                            nc.scalar.activation(
                                out=half_abs[:],
                                in_=feat_t[:, N_VEC + step, :],
                                func=ACT.Abs,
                                bias=proto_act_half[:, step, p : p + 1],
                                scale=-0.5,
                            )
                            add_turned(nc, ident_f32, turned, half_abs, first=(step == 0), last=False)
                    if step < n_turn:
                        for p, vec_tiles, turned in waiting:
                            add_turned(nc, ident_f32, turned, vec_tiles[step], first=False, last=(step == n_turn - 1))

                if pair == 2:
                    add_turned(nc, ident_f32, feat_turned, feat_sum, first=True, last=True)

                for p, vec_tiles, turned in closed:
                    nc.vector.tensor_reduce(out=half_sum[:, p, :], in_=turned[:], axis=AXIS.X, op=ALU.add)
                if current:
                    n_chain = N_CHAIN + 1 if pair % PERIOD == 0 else N_CHAIN
                    n_plain = N_VEC - n_chain
                    slot = pair % N_SLOT
                    work_a = sum_pool.tile([P, B], F32, tag="work_a")
                    work_b = swap_pool.tile([P, B], F32, tag="work_b%d" % slot, offset=slot * B * 4)
                    work = [work_a, work_b]
                    sum_a = sum_pool.tile([P, B], F32, tag="sum_a")
                    sum_b = sum_pool.tile([P, B], F32, tag="sum_b")
                    final = [sum_a, sum_b]
                    plain = [[], []]
                    order = []
                    for back in range(max(n_chain, n_plain)):
                        if back < n_chain:
                            order.append(("chain", n_chain - 1 - back))
                        if back < n_plain:
                            order.append(("plain", n_plain - 1 - back))
                    for what, n in reversed(order):
                        for i in range(2):
                            p = current[i][0]
                            if what == "plain" and i == 0 and n == n_plain - 1:
                                pass
                            elif what == "plain":
                                max_alone = alone_pool.tile([P, B], F32)
                                nc.vector.tensor_scalar(
                                    out=max_alone[:],
                                    in0=feat_t[:, n_chain + n, :],
                                    scalar1=proto_vec[:, n_chain + n, p : p + 1],
                                    scalar2=None,
                                    op0=ALU.max,
                                )
                                plain[i].append(max_alone)
                            elif n == 0:
                                nc.vector.tensor_scalar(
                                    out=work[i][:],
                                    in0=feat_t[:, 0, :],
                                    scalar1=proto_vec[:, 0, p : p + 1],
                                    scalar2=proto_neg_half_sum[:, p : p + 1],
                                    op0=ALU.max,
                                    op1=ALU.add,
                                )
                            else:
                                target = final[i] if n == n_chain - 1 else work[i]
                                nc.vector.scalar_tensor_tensor(
                                    out=target[:],
                                    in0=feat_t[:, n, :],
                                    scalar=proto_vec[:, n, p : p + 1],
                                    in1=work[i][:],
                                    op0=ALU.max,
                                    op1=ALU.add,
                                )
                    max_pool = swap_pool.tile([P, B], F32, tag="max_pool%d" % slot, offset=slot * B * 4)
                    nc.gpsimd.tensor_scalar(
                        out=max_pool[:],
                        in0=feat_t[:, N_VEC - 1, :],
                        scalar1=proto_vec[:, N_VEC - 1, current[0][0] : current[0][0] + 1],
                        scalar2=0.0,
                        op0=ALU.max,
                        op1=ALU.add,
                    )
                    for i in range(2):
                        current[i][1].extend(plain[i] + [final[i]])
                    current[0][1].append(max_pool)
                closed = waiting
                waiting = current

        feat_rowsum = small.tile([P, N_BT], F32)
        nc.vector.tensor_reduce(out=feat_rowsum[:], in_=feat_turned[:], axis=AXIS.X, op=ALU.add)
        result = small.tile([P, N_BT, N_PROTO], F32)
        for bt in range(N_BT):
            nc.vector.tensor_scalar(
                out=result[:, bt, :],
                in0=half_sum[:, :, bt],
                scalar1=-2.0,
                scalar2=feat_rowsum[:, bt : bt + 1],
                op0=ALU.mult,
                op1=ALU.add,
            )
        nc.sync.dma_start(out=out.rearrange("(t b) p -> b t p", b=P), in_=result[:])


def tile_prototypelearnerv4_pa_kernel(
    tc, x, aW_words, aW_scales, ab, h_up, h_skip, Wu2_words, Wu2_scales, bu2, Wu3_words, Wu3_scales, bu3, protos, out
):
    nc = tc.nc
    with tc.tile_pool(name="keep", bufs=1) as keep:
        ident_f32 = keep.tile([P, P], F32)
        make_identity(nc, ident_f32[:])
        feat_t = keep.tile([P, N_CHUNK, B], F32)
        feat_sum = keep.tile([P, B], F32)
        proto_vec = keep.tile([P, N_VEC, N_PROTO], F32)
        proto_act_half = keep.tile([P, N_ACT, N_PROTO], F32)
        proto_neg_half_sum = keep.tile([P, N_PROTO], F32)
        ins = (x, aW_words, aW_scales, ab, h_up, h_skip, Wu2_words, Wu2_scales, bu2, Wu3_words, Wu3_scales, bu3, protos)
        with tc.psum_pool(name="psum", bufs=1) as psum, tc.tile_pool(name="act_pool", bufs=16) as act_pool:
            build_features(tc, psum, ins, ident_f32, feat_t, feat_sum, proto_vec, proto_act_half, proto_neg_half_sum)
            sum_distances(tc, psum, act_pool, ident_f32, feat_t, feat_sum, proto_vec, proto_act_half, proto_neg_half_sum, out)
